import numpy as np
import ml_dtypes


def mxq(x, axis, fmt="e4m3"):
    dtype, down = {"e4m3": (ml_dtypes.float8_e4m3fn, 7), "e5m2": (ml_dtypes.float8_e5m2, 14)}[fmt]
    v = np.moveaxis(np.asarray(x, np.float32).astype(ml_dtypes.bfloat16).astype(np.float64), axis, -1)
    blocks = v.reshape(v.shape[:-1] + (-1, 32))
    amax = np.abs(blocks).max(-1, keepdims=True)
    byte = np.maximum(np.where(amax > 0, np.frexp(amax)[1] - 1 + 127, 0) - down, 1)
    scale = np.exp2(byte - 127.0)
    codes = (blocks / scale).astype(np.float32).astype(dtype).astype(np.float64)
    return np.moveaxis((codes * scale).reshape(v.shape), -1, axis)


WIDE = False


def mx_kscale(k):
    if not WIDE:
        return np.ones(k)
    levels = np.array([10, -10, 5, -5, 0])
    a = np.random.permutation(np.resize(levels, k // 512 * 4)).reshape(k // 512, 4)
    idx = np.arange(k)
    return np.exp2(a[idx // 512, idx % 128 // 32])


BF16 = ml_dtypes.bfloat16


def bf(x):
    return np.asarray(x, np.float32).astype(BF16)


def f64(x):
    return np.asarray(x).astype(np.float64)


B, S, D = 4, 1024, 512
SCALE = 1.0 / np.sqrt(D)


def setup_inputs():
    s = mx_kscale(D)
    return {"x1": bf(np.random.standard_normal((B, S, D)) * 2.0 * s), "x2": bf(np.random.standard_normal((B, S, D)) / s)}


def reference(x1, x2):
    x2 = f64(x2)
    scores = (mxq(f64(x1), 2, "e4m3") @ mxq(x2, 2, "e4m3").transpose(0, 2, 1)) * SCALE
    e = np.exp(scores - scores.max(-1, keepdims=True))
    return (mxq(e, 2, "e4m3") @ mxq(x2, 1, "e4m3")) / e.sum(-1, keepdims=True)

@@ -1,0 +1,288 @@
+from contextlib import ExitStack
+import math
+
+import concourse.mybir as mybir
+from concourse.masks import make_identity
+
+F32 = mybir.dt.float32
+BF16 = mybir.dt.bfloat16
+U32 = mybir.dt.uint32
+U8 = mybir.dt.uint8
+FP8X4 = mybir.dt.float8_e4m3fn_x4
+ACTF = mybir.ActivationFunctionType
+ALU = mybir.AluOpType
+AX = mybir.AxisListType
+
+B, S, D = 4, 1024, 512
+P = 128
+NT = S // P
+NQ = B * NT
+SCALE = 1.0 / math.sqrt(D)
+FLOPS = 2 * 2 * B * S * S * D
+
+MANUAL = True
+H_ON_VECTOR = ()
+
+
+def tile_model_t_kernel(tc, x1, x2, out):
+    nc = tc.nc
+    with ExitStack() as ctx:
+        if MANUAL:
+            ctx.enter_context(tc.manual_schedule())
+        const = ctx.enter_context(tc.tile_pool(name="const", bufs=1))
+        xin = ctx.enter_context(tc.tile_pool(name="xin", bufs=1))
+        prep = ctx.enter_context(tc.tile_pool(name="prep", bufs=2))
+        work = ctx.enter_context(tc.tile_pool(name="work", bufs=4))
+        small = ctx.enter_context(tc.tile_pool(name="small", bufs=6))
+        ps_s = ctx.enter_context(tc.psum_pool(name="ps_s", bufs=2))
+        ps_t = ctx.enter_context(tc.psum_pool(name="ps_t", bufs=2))
+        ps_o = ctx.enter_context(tc.psum_pool(name="ps_o", bufs=1))
+        ps_x = ctx.enter_context(tc.psum_pool(name="ps_x", bufs=1))
+
+        x1_sb = []
+        x2_sb = []
+        for b in range(B):
+            t2 = xin.tile([P, NT, D], BF16, name="x2_sb%d" % b)
+            t1 = xin.tile([P, NT, D], BF16, name="x1_sb%d" % b)
+            x2_sb.append(t2)
+            x1_sb.append(t1)
+        for b in range(B):
+            v2 = x2[b].rearrange("(g p t) d -> p g t d", g=2, t=4)
+            v1 = x1[b].rearrange("(p c) d -> p c d", c=NT)
+            if b == 0:
+                nc.sync.dma_start(out=x2_sb[b][:, 0:4, :], in_=v2[:, 0])
+                nc.sync.dma_start(out=x1_sb[b][:, 0:2, :], in_=v1[:, 0:2, :])
+                nc.sync.dma_start(out=x2_sb[b][:, 4:8, :], in_=v2[:, 1])
+                nc.sync.dma_start(out=x1_sb[b][:, 2:8, :], in_=v1[:, 2:8, :])
+            else:
+                nc.sync.dma_start(out=x2_sb[b][:, 0:4, :], in_=v2[:, 0])
+                nc.sync.dma_start(out=x2_sb[b][:, 4:8, :], in_=v2[:, 1])
+                nc.sync.dma_start(out=x1_sb[b][:], in_=v1)
+        out_v = [out[b].rearrange("(p c) d -> p c d", c=NT) for b in range(B)]
+
+        ident_f = const.tile([P, P], F32, name="ident_f")
+        make_identity(nc, ident_f[:])
+        ident_b = const.tile([P, P], BF16, name="ident_b")
+        make_identity(nc, ident_b[:])
+
+        ops = {}
+        SHAPES = {
+            "g1": ([P, 4 * S], BF16), "g2": ([P, 4 * S], BF16), "gv": ([P, 2, D, 4], BF16),
+            "c1": ([P, S], U32), "c2": ([P, S], U32), "cv": ([P, 2, D], U32),
+            "s1": ([P, S], U8), "s2": ([P, S], U8), "sv": ([P, 2, D], U8),
+        }
+
+        def op(b, key):
+            if (b, key) not in ops:
+                shape, dt = SHAPES[key]
+                ops[(b, key)] = prep.tile(shape, dt, name=key, align_bytes=64)
+            return ops[(b, key)]
+
+        xts = {}
+
+        def prep_t(b, which, k, pool, tag):
+            src = x1_sb[b] if which == 1 else x2_sb[b]
+            xt = pool.tile([P, 2, 2, P], F32, name="xt", tag=tag)
+            for r in range(2):
+                words = src[:, 2 * k + r, :].bitcast(F32)
+                for u in range(2):
+                    nc.tensor.transpose(xt[:, r, u, :], words[:, P * u:P * (u + 1)], ident_f[:])
+            xts[(b, which, k)] = xt
+
+        def prep_e(b, which, k, eng):
+            xt = xts[(b, which, k)]
+            grouped = op(b, "g%d" % which)
+            dst = grouped[:, 1024 * k:1024 * (k + 1)].bitcast(F32).rearrange("p (r j u) -> p r j u", r=2, u=2)
+            srcv = xt[:].rearrange("p r u j -> p r j u")
+            if eng == "v":
+                nc.vector.tensor_copy(out=dst, in_=srcv)
+            else:
+                nc.scalar.copy(out=dst, in_=srcv)
+
+        def prep_q(b, which, k):
+            nc.vector.quantize_mx(
+                out=op(b, "c%d" % which)[:, 256 * k:256 * (k + 1)].bitcast(FP8X4),
+                scales=op(b, "s%d" % which)[:, 256 * k:256 * (k + 1)],
+                in_=op(b, "g%d" % which)[:, 1024 * k:1024 * (k + 1)],
+            )
+
+        def prep_vc(b, j, w):
+            g, lo = divmod(j * w, D)
+            nc.vector.tensor_copy(
+                out=op(b, "gv")[:, g, lo:lo + w, :].rearrange("p (c i) t -> p c t i", i=4),
+                in_=x2_sb[b][:, 4 * g:4 * g + 4, lo:lo + w].rearrange("p t (c i) -> p c t i", i=4),
+            )
+
+        def prep_vq(b, j, w):
+            g, lo = divmod(j * w, D)
+            nc.vector.quantize_mx(
+                out=op(b, "cv")[:, g, lo:lo + w].bitcast(FP8X4),
+                scales=op(b, "sv")[:, g, lo:lo + w],
+                in_=op(b, "gv")[:, g, lo:lo + w, :].rearrange("p d t -> p (d t)"),
+            )
+
+        st = {}
+
+        def stage_a(i):
+            if not 0 <= i < NQ:
+                return
+            b, c = divmod(i, NT)
+            s = []
+            for h in range(2):
+                sh = ps_s.tile([P, 512], F32, name="s%d" % h, tag="S%d" % h)
+                nc.tensor.matmul_mx(
+                    out=sh[:],
+                    lhsT=op(b, "c1")[:, P * c:P * (c + 1)].bitcast(FP8X4),
+                    lhsT_scale=op(b, "s1")[:, P * c:P * (c + 1)],
+                    rhs=op(b, "c2")[:, 512 * h:512 * (h + 1)].bitcast(FP8X4),
+                    rhs_scale=op(b, "s2")[:, 512 * h:512 * (h + 1)],
+                    start=True,
+                    stop=True,
+                )
+                s.append(sh)
+            st[("s", i)] = s
+
+        def stage_b(i):
+            if not 0 <= i < NQ:
+                return
+            s = st[("s", i)]
+            mx = small.tile([P, 2], F32, name="mx")
+            for h in range(2):
+                nc.vector.reduce_max(out=mx[:, h:h + 1], in_=s[h][:], axis=AX.X)
+            nm = small.tile([P, 1], F32, name="nm")
+            nc.vector.tensor_scalar(out=nm[:], in0=mx[:, 0:1], scalar1=mx[:, 1:2], scalar2=-SCALE,
+                                    op0=ALU.max, op1=ALU.mult)
+            st[("nm", i)] = nm
+
+        def stage_c(i):
+            if not 0 <= i < NQ:
+                return
+            s = st[("s", i)]
+            nm = st[("nm", i)]
+            e = work.tile([P, S], BF16, name="e")
+            sm = small.tile([P, 2], F32, name="sm")
+            for h in range(2):
+                nc.scalar.activation(out=e[:, 512 * h:512 * (h + 1)], in_=s[h][:], func=ACTF.Exp,
+                                     bias=nm[:], scale=SCALE, accum_out=sm[:, h:h + 1])
+            st[("e", i)] = e
+            st[("sm", i)] = sm
+
+        def stage_d(i):
+            if not 0 <= i < NQ:
+                return
+            e = st[("e", i)]
+            et = ps_t.tile([P, NT, P], BF16, name="et", tag="T")
+            for c in range(NT):
+                nc.tensor.transpose(et[:, c, :], e[:, P * c:P * (c + 1)], ident_b[:])
+            st[("et", i)] = et
+
+        def stage_e(i):
+            if not 0 <= i < NQ:
+                return
+            et = st[("et", i)]
+            eg = work.tile([P, 2, P, 4], BF16, name="eg", align_bytes=64)
+            nc.scalar.copy(out=eg[:], in_=et[:].rearrange("p (g t) q -> p g q t", g=2))
+            st[("eg", i)] = eg
+
+        def stage_f(i):
+            if not 0 <= i < NQ:
+                return
+            eg = st[("eg", i)]
+            ec = work.tile([P, 2 * P], U32, name="ec", align_bytes=64)
+            es = work.tile([P, 2 * P], U8, name="es", align_bytes=64)
+            nc.vector.quantize_mx(out=ec[:].bitcast(FP8X4), scales=es[:],
+                                  in_=eg[:].rearrange("p g q t -> p (g q t)"))
+            st[("ec", i)] = (ec, es)
+
+        def stage_r(i):
+            if not 0 <= i < NQ:
+                return
+            sm = st[("sm", i)]
+            tot = small.tile([P, 1], F32, name="tot")
+            nc.vector.tensor_tensor(out=tot[:], in0=sm[:, 0:1], in1=sm[:, 1:2], op=ALU.add)
+            rs = small.tile([P, 1], F32, name="rs")
+            nc.vector.reciprocal(out=rs[:], in_=tot[:])
+            st[("rs", i)] = rs
+
+        def stage_g(i):
+            if not 0 <= i < NQ:
+                return
+            b, c = divmod(i, NT)
+            ec, es = st[("ec", i)]
+            o = ps_o.tile([P, D], F32, name="o", tag="O")
+            for g in range(2):
+                nc.tensor.matmul_mx(
+                    out=o[:],
+                    lhsT=ec[:, P * g:P * (g + 1)].bitcast(FP8X4),
+                    lhsT_scale=es[:, P * g:P * (g + 1)],
+                    rhs=op(b, "cv")[:, g, :].bitcast(FP8X4),
+                    rhs_scale=op(b, "sv")[:, g, :],
+                    start=(g == 0),
+                    stop=(g == 1),
+                )
+            st[("o", i)] = o
+
+        def stage_h(i):
+            if not 0 <= i < NQ:
+                return
+            b, c = divmod(i, NT)
+            o = st[("o", i)]
+            rs = st[("rs", i)]
+            if c % 2 == 0:
+                st["osb"] = work.tile([P, 2, D], F32, name="osb")
+            osb = st["osb"]
+            if c in H_ON_VECTOR:
+                nc.vector.tensor_scalar(out=osb[:, c % 2, :], in0=o[:], scalar1=rs[:], scalar2=None, op0=ALU.mult)
+            else:
+                nc.scalar.activation(out=osb[:, c % 2, :], in_=o[:], func=ACTF.Copy, scale=rs[:])
+            if c % 2 == 1:
+                nc.sync.dma_start(out=out_v[b][:, c - 1:c + 1, :], in_=osb[:])
+
+        PIECES = [(2, 0), (2, 1), (2, 2), (2, 3), (1, 0), (1, 1), (1, 2), (1, 3)]
+
+        def piece(n):
+            b, c = divmod(n, NT)
+            if n < 0 or b + 1 >= B:
+                return None
+            return (b + 1,) + PIECES[c]
+
+        order0 = [(2, 0, ps_t, "T"), (2, 1, ps_t, "T"), (1, 0, ps_o, "O"), (2, 2, ps_s, "S0"), (2, 3, ps_s, "S1"),
+                  (1, 1, ps_x, "X"), (1, 2, ps_s, "S0"), (1, 3, ps_s, "S1")]
+        for idx, (which, k, pool, tag) in enumerate(order0):
+            prep_t(0, which, k, pool, tag)
+        for idx, (which, k, pool, tag) in enumerate(order0):
+            prep_e(0, which, k, "v" if idx % 2 == 0 else "s")
+            if idx >= 2:
+                prep_q(0, order0[idx - 2][0], order0[idx - 2][1])
+        for idx in (6, 7):
+            prep_q(0, order0[idx][0], order0[idx][1])
+
+        VW = 128
+        for n in range(-1, NQ + 2):
+            b, c = divmod(n, NT)
+            pp = piece(n - 1)
+            pn = piece(n)
+            stage_g(n - 2)
+            stage_a(n + 1)
+            stage_c(n)
+            stage_b(n + 1)
+            stage_d(n)
+            stage_e(n - 1)
+            stage_f(n - 1)
+            stage_r(n - 1)
+            if pn is not None:
+                prep_t(pn[0], pn[1], pn[2], ps_x, "X")
+            stage_h(n - 2)
+            if pn is not None:
+                prep_e(pn[0], pn[1], pn[2], "v")
+            if pp is not None:
+                prep_q(pp[0], pp[1], pp[2])
+            if n == -1:
+                for j in range(2):
+                    prep_vc(0, j, 512)
+                for j in range(2):
+                    prep_vq(0, j, 512)
+            if pn is not None:
+                prep_vc(pn[0], c, VW)
+            if pp is not None:
+                prep_vq(pp[0], (c - 1) % NT, VW)

@@ -50,9 +50,11 @@ def tile_model_t_kernel(tc, x1, x2, out):
             v2 = x2[b].rearrange("(g p t) d -> p g t d", g=2, t=4)
             v1 = x1[b].rearrange("(p c) d -> p c d", c=NT)
             if b == 0:
-                nc.sync.dma_start(out=x2_sb[b][:, 0:4, :], in_=v2[:, 0])
+                nc.sync.dma_start(out=x2_sb[b][:, 0:2, :], in_=v2[:, 0, 0:2, :])
+                nc.sync.dma_start(out=x2_sb[b][:, 2:4, :], in_=v2[:, 0, 2:4, :])
                 nc.sync.dma_start(out=x1_sb[b][:, 0:2, :], in_=v1[:, 0:2, :])
-                nc.sync.dma_start(out=x2_sb[b][:, 4:8, :], in_=v2[:, 1])
+                nc.sync.dma_start(out=x2_sb[b][:, 4:6, :], in_=v2[:, 1, 0:2, :])
+                nc.sync.dma_start(out=x2_sb[b][:, 6:8, :], in_=v2[:, 1, 2:4, :])
                 nc.sync.dma_start(out=x1_sb[b][:, 2:8, :], in_=v1[:, 2:8, :])
             else:
                 nc.sync.dma_start(out=x2_sb[b][:, 0:4, :], in_=v2[:, 0])
@@ -106,12 +108,14 @@ def tile_model_t_kernel(tc, x1, x2, out):
                 in_=op(b, "g%d" % which)[:, 1024 * k:1024 * (k + 1)],
             )
 
-        def prep_vc(b, j, w):
+        def prep_vc(b, j, w, eng="v"):
             g, lo = divmod(j * w, D)
-            nc.vector.tensor_copy(
-                out=op(b, "gv")[:, g, lo:lo + w, :].rearrange("p (c i) t -> p c t i", i=4),
-                in_=x2_sb[b][:, 4 * g:4 * g + 4, lo:lo + w].rearrange("p t (c i) -> p c t i", i=4),
-            )
+            dst = op(b, "gv")[:, g, lo:lo + w, :].rearrange("p (c i) t -> p c t i", i=4)
+            srcv = x2_sb[b][:, 4 * g:4 * g + 4, lo:lo + w].rearrange("p t (c i) -> p c t i", i=4)
+            if eng == "v":
+                nc.vector.tensor_copy(out=dst, in_=srcv)
+            else:
+                nc.scalar.copy(out=dst, in_=srcv)
 
         def prep_vq(b, j, w):
             g, lo = divmod(j * w, D)
@@ -160,12 +164,13 @@ def tile_model_t_kernel(tc, x1, x2, out):
             s = st[("s", i)]
             nm = st[("nm", i)]
             e = work.tile([P, S], BF16, name="e")
-            sm = small.tile([P, 2], F32, name="sm")
+            if i % 2 == 0:
+                st[("sm", i // 2)] = small.tile([P, 2, 2], F32, name="sm")
+            sm = st[("sm", i // 2)]
             for h in range(2):
                 nc.scalar.activation(out=e[:, 512 * h:512 * (h + 1)], in_=s[h][:], func=ACTF.Exp,
-                                     bias=nm[:], scale=SCALE, accum_out=sm[:, h:h + 1])
+                                     bias=nm[:], scale=SCALE, accum_out=sm[:, i % 2, h:h + 1])
             st[("e", i)] = e
-            st[("sm", i)] = sm
 
         def stage_d(i):
             if not 0 <= i < NQ:
@@ -195,14 +200,14 @@ def tile_model_t_kernel(tc, x1, x2, out):
             st[("ec", i)] = (ec, es)
 
         def stage_r(i):
-            if not 0 <= i < NQ:
+            if not 0 <= i < NQ or i % 2 == 0:
                 return
-            sm = st[("sm", i)]
-            tot = small.tile([P, 1], F32, name="tot")
-            nc.vector.tensor_tensor(out=tot[:], in0=sm[:, 0:1], in1=sm[:, 1:2], op=ALU.add)
-            rs = small.tile([P, 1], F32, name="rs")
+            sm = st[("sm", i // 2)]
+            tot = small.tile([P, 2], F32, name="tot")
+            nc.vector.reduce_sum(out=tot[:], in_=sm[:], axis=AX.X)
+            rs = small.tile([P, 2], F32, name="rs")
             nc.vector.reciprocal(out=rs[:], in_=tot[:])
-            st[("rs", i)] = rs
+            st[("rs", i // 2)] = rs
 
         def stage_g(i):
             if not 0 <= i < NQ:
@@ -227,62 +232,75 @@ def tile_model_t_kernel(tc, x1, x2, out):
                 return
             b, c = divmod(i, NT)
             o = st[("o", i)]
-            rs = st[("rs", i)]
+            rs = st[("rs", i // 2)][:, c % 2:c % 2 + 1]
             if c % 2 == 0:
                 st["osb"] = work.tile([P, 2, D], F32, name="osb")
             osb = st["osb"]
             if c in H_ON_VECTOR:
-                nc.vector.tensor_scalar(out=osb[:, c % 2, :], in0=o[:], scalar1=rs[:], scalar2=None, op0=ALU.mult)
+                nc.vector.tensor_scalar(out=osb[:, c % 2, :], in0=o[:], scalar1=rs, scalar2=None, op0=ALU.mult)
             else:
-                nc.scalar.activation(out=osb[:, c % 2, :], in_=o[:], func=ACTF.Copy, scale=rs[:])
-            if c % 2 == 1:
+                nc.scalar.activation(out=osb[:, c % 2, :], in_=o[:], func=ACTF.Copy, scale=rs)
+            if i >= NQ - 2:
+                nc.sync.dma_start(out=out_v[b][:, c, :], in_=osb[:, c % 2, :])
+            elif c % 2 == 1:
                 nc.sync.dma_start(out=out_v[b][:, c - 1:c + 1, :], in_=osb[:])
 
         PIECES = [(2, 0), (2, 1), (2, 2), (2, 3), (1, 0), (1, 1), (1, 2), (1, 3)]
 
         def piece(n):
-            b, c = divmod(n, NT)
-            if n < 0 or b + 1 >= B:
+            if -2 <= n <= 0:
+                return (0, 1, n + 3, None)
+            b, j = divmod(n - 1, NT)
+            if n < 1 or b + 1 >= B:
                 return None
-            return (b + 1,) + PIECES[c]
+            return (b + 1,) + PIECES[j] + (j,)
 
-        order0 = [(2, 0, ps_t, "T"), (2, 1, ps_t, "T"), (1, 0, ps_o, "O"), (2, 2, ps_s, "S0"), (2, 3, ps_s, "S1"),
-                  (1, 1, ps_x, "X"), (1, 2, ps_s, "S0"), (1, 3, ps_s, "S1")]
-        for idx, (which, k, pool, tag) in enumerate(order0):
-            prep_t(0, which, k, pool, tag)
-        for idx, (which, k, pool, tag) in enumerate(order0):
-            prep_e(0, which, k, "v" if idx % 2 == 0 else "s")
-            if idx >= 2:
-                prep_q(0, order0[idx - 2][0], order0[idx - 2][1])
-        for idx in (6, 7):
-            prep_q(0, order0[idx][0], order0[idx][1])
+        prep_t(0, 2, 0, ps_t, "T")
+        prep_t(0, 2, 1, ps_t, "T")
+        prep_t(0, 1, 0, ps_o, "O")
+        prep_t(0, 2, 2, ps_s, "S0")
+        prep_t(0, 2, 3, ps_s, "S1")
+        prep_vc(0, 0, 512, "v")
+        prep_e(0, 2, 0, "s")
+        prep_e(0, 2, 1, "v")
+        prep_e(0, 1, 0, "s")
+        prep_q(0, 2, 0)
+        prep_q(0, 2, 1)
+        prep_q(0, 1, 0)
+        prep_e(0, 2, 2, "s")
+        prep_e(0, 2, 3, "s")
+        prep_vc(0, 1, 512, "s")
+        prep_q(0, 2, 2)
+        prep_q(0, 2, 3)
 
         VW = 128
-        for n in range(-1, NQ + 2):
-            b, c = divmod(n, NT)
-            pp = piece(n - 1)
+        for n in range(-2, 0):
             pn = piece(n)
+            stage_a(n + 2)
+            stage_b(n + 2)
+            prep_t(pn[0], pn[1], pn[2], ps_x, "X")
+            prep_e(pn[0], pn[1], pn[2], "v")
+            prep_vq(0, n + 2, 512)
+            prep_q(pn[0], pn[1], pn[2])
+        for n in range(0, NQ + 2):
+            pn = piece(n)
+            pp = piece(n - 1)
             stage_g(n - 2)
-            stage_a(n + 1)
+            if pn is not None:
+                prep_t(pn[0], pn[1], pn[2], ps_x, "X")
             stage_c(n)
-            stage_b(n + 1)
+            stage_a(n + 2)
             stage_d(n)
+            if pn is not None:
+                prep_e(pn[0], pn[1], pn[2], "v")
             stage_e(n - 1)
             stage_f(n - 1)
             stage_r(n - 1)
-            if pn is not None:
-                prep_t(pn[0], pn[1], pn[2], ps_x, "X")
             stage_h(n - 2)
+            stage_b(n + 2)
             if pn is not None:
-                prep_e(pn[0], pn[1], pn[2], "v")
-            if pp is not None:
-                prep_q(pp[0], pp[1], pp[2])
-            if n == -1:
-                for j in range(2):
-                    prep_vc(0, j, 512)
-                for j in range(2):
-                    prep_vq(0, j, 512)
-            if pn is not None:
-                prep_vc(pn[0], c, VW)
-            if pp is not None:
-                prep_vq(pp[0], (c - 1) % NT, VW)
+                prep_q(pn[0], pn[1], pn[2])
+            if pn is not None and pn[3] is not None:
+                prep_vc(pn[0], pn[3], VW)
+            if pp is not None and pp[3] is not None:
+                prep_vq(pp[0], pp[3], VW)

@@ -21,7 +21,8 @@ SCALE = 1.0 / math.sqrt(D)
 FLOPS = 2 * 2 * B * S * S * D
 
 MANUAL = True
-H_ON_VECTOR = ()
+H_VECTOR_FROM = 24
+PE_ON_SCALAR = (3,)
 
 
 def tile_model_t_kernel(tc, x1, x2, out):
@@ -164,13 +165,12 @@ def tile_model_t_kernel(tc, x1, x2, out):
             s = st[("s", i)]
             nm = st[("nm", i)]
             e = work.tile([P, S], BF16, name="e")
-            if i % 2 == 0:
-                st[("sm", i // 2)] = small.tile([P, 2, 2], F32, name="sm")
-            sm = st[("sm", i // 2)]
+            sm = small.tile([P, 2], F32, name="sm")
             for h in range(2):
                 nc.scalar.activation(out=e[:, 512 * h:512 * (h + 1)], in_=s[h][:], func=ACTF.Exp,
-                                     bias=nm[:], scale=SCALE, accum_out=sm[:, i % 2, h:h + 1])
+                                     bias=nm[:], scale=SCALE, accum_out=sm[:, h:h + 1])
             st[("e", i)] = e
+            st[("sm", i)] = sm
 
         def stage_d(i):
             if not 0 <= i < NQ:
@@ -200,14 +200,14 @@ def tile_model_t_kernel(tc, x1, x2, out):
             st[("ec", i)] = (ec, es)
 
         def stage_r(i):
-            if not 0 <= i < NQ or i % 2 == 0:
+            if not 0 <= i < NQ:
                 return
-            sm = st[("sm", i // 2)]
-            tot = small.tile([P, 2], F32, name="tot")
-            nc.vector.reduce_sum(out=tot[:], in_=sm[:], axis=AX.X)
-            rs = small.tile([P, 2], F32, name="rs")
+            sm = st[("sm", i)]
+            tot = small.tile([P, 1], F32, name="tot")
+            nc.vector.tensor_tensor(out=tot[:], in0=sm[:, 0:1], in1=sm[:, 1:2], op=ALU.add)
+            rs = small.tile([P, 1], F32, name="rs")
             nc.vector.reciprocal(out=rs[:], in_=tot[:])
-            st[("rs", i // 2)] = rs
+            st[("rs", i)] = rs
 
         def stage_g(i):
             if not 0 <= i < NQ:
@@ -227,16 +227,16 @@ def tile_model_t_kernel(tc, x1, x2, out):
                 )
             st[("o", i)] = o
 
-        def stage_h(i):
-            if not 0 <= i < NQ:
+        def stage_h(i, eng):
+            if not 0 <= i < NQ or eng != ("v" if i >= H_VECTOR_FROM else "s"):
                 return
             b, c = divmod(i, NT)
             o = st[("o", i)]
-            rs = st[("rs", i // 2)][:, c % 2:c % 2 + 1]
+            rs = st[("rs", i)][:]
             if c % 2 == 0:
                 st["osb"] = work.tile([P, 2, D], F32, name="osb")
             osb = st["osb"]
-            if c in H_ON_VECTOR:
+            if eng == "v":
                 nc.vector.tensor_scalar(out=osb[:, c % 2, :], in0=o[:], scalar1=rs, scalar2=None, op0=ALU.mult)
             else:
                 nc.scalar.activation(out=osb[:, c % 2, :], in_=o[:], func=ACTF.Copy, scale=rs)
@@ -274,33 +274,28 @@ def tile_model_t_kernel(tc, x1, x2, out):
         prep_q(0, 2, 3)
 
         VW = 128
-        for n in range(-2, 0):
-            pn = piece(n)
-            stage_a(n + 2)
-            stage_b(n + 2)
-            prep_t(pn[0], pn[1], pn[2], ps_x, "X")
-            prep_e(pn[0], pn[1], pn[2], "v")
-            prep_vq(0, n + 2, 512)
-            prep_q(pn[0], pn[1], pn[2])
-        for n in range(0, NQ + 2):
+        for n in range(-2, NQ + 3):
             pn = piece(n)
             pp = piece(n - 1)
             stage_g(n - 2)
-            if pn is not None:
-                prep_t(pn[0], pn[1], pn[2], ps_x, "X")
             stage_c(n)
+            stage_r(n - 1)
+            if pp is not None:
+                prep_e(pp[0], pp[1], pp[2], "s" if pp[3] in PE_ON_SCALAR else "v")
+            stage_h(n - 2, "v")
+            if pp is not None and pp[3] is not None:
+                prep_vq(pp[0], pp[3], VW)
+            if n == -1 or n == 0:
+                prep_vq(0, n + 1, 512)
+            if pn is not None and pn[3] is not None:
+                prep_vc(pn[0], pn[3], VW)
+            if pp is not None:
+                prep_q(pp[0], pp[1], pp[2])
             stage_a(n + 2)
             stage_d(n)
             if pn is not None:
-                prep_e(pn[0], pn[1], pn[2], "v")
+                prep_t(pn[0], pn[1], pn[2], ps_x, "X")
             stage_e(n - 1)
             stage_f(n - 1)
-            stage_r(n - 1)
-            stage_h(n - 2)
+            stage_h(n - 2, "s")
             stage_b(n + 2)
-            if pn is not None:
-                prep_q(pn[0], pn[1], pn[2])
-            if pn is not None and pn[3] is not None:
-                prep_vc(pn[0], pn[3], VW)
-            if pp is not None and pp[3] is not None:
-                prep_vq(pp[0], pp[3], VW)

@@ -22,7 +22,7 @@ FLOPS = 2 * 2 * B * S * S * D
 
 MANUAL = True
 H_VECTOR_FROM = 24
-PE_ON_SCALAR = (3,)
+PE_ON_SCALAR = ()
 
 
 def tile_model_t_kernel(tc, x1, x2, out):
@@ -115,8 +115,14 @@ def tile_model_t_kernel(tc, x1, x2, out):
             srcv = x2_sb[b][:, 4 * g:4 * g + 4, lo:lo + w].rearrange("p t (c i) -> p c t i", i=4)
             if eng == "v":
                 nc.vector.tensor_copy(out=dst, in_=srcv)
-            else:
+            elif eng == "s":
                 nc.scalar.copy(out=dst, in_=srcv)
+            else:
+                nc.gpsimd.tensor_scalar(
+                    out=op(b, "gv")[:, g, lo:lo + w, :],
+                    in0=x2_sb[b][:, 4 * g:4 * g + 4, lo:lo + w].rearrange("p t d -> p d t"),
+                    scalar1=1.0, scalar2=0.0, op0=ALU.mult, op1=ALU.add,
+                )
 
         def prep_vq(b, j, w):
             g, lo = divmod(j * w, D)
@@ -199,12 +205,24 @@ def tile_model_t_kernel(tc, x1, x2, out):
                                   in_=eg[:].rearrange("p g q t -> p (g q t)"))
             st[("ec", i)] = (ec, es)
 
-        def stage_r(i):
+        def stage_tot(i):
             if not 0 <= i < NQ:
                 return
             sm = st[("sm", i)]
             tot = small.tile([P, 1], F32, name="tot")
-            nc.vector.tensor_tensor(out=tot[:], in0=sm[:, 0:1], in1=sm[:, 1:2], op=ALU.add)
+            nc.gpsimd.tensor_tensor(out=tot[:], in0=sm[:, 0:1], in1=sm[:, 1:2], op=ALU.add)
+            st[("tot", i)] = tot
+
+        def token(i):
+            if not 0 <= i < NQ:
+                return
+            tok = small.tile([P, 1], F32, name="tok")
+            nc.gpsimd.tensor_copy(out=tok[:], in_=st[("rs", i)][:])
+
+        def stage_r(i):
+            if not 0 <= i < NQ:
+                return
+            tot = st[("tot", i)]
             rs = small.tile([P, 1], F32, name="rs")
             nc.vector.reciprocal(out=rs[:], in_=tot[:])
             st[("rs", i)] = rs
@@ -214,7 +232,10 @@ def tile_model_t_kernel(tc, x1, x2, out):
                 return
             b, c = divmod(i, NT)
             ec, es = st[("ec", i)]
-            o = ps_o.tile([P, D], F32, name="o", tag="O")
+            if i >= 25 and i % 2 == 1:
+                o = ps_x.tile([P, D], F32, name="o", tag="X")
+            else:
+                o = ps_o.tile([P, D], F32, name="o", tag="O")
             for g in range(2):
                 nc.tensor.matmul_mx(
                     out=o[:],
@@ -248,10 +269,10 @@ def tile_model_t_kernel(tc, x1, x2, out):
         PIECES = [(2, 0), (2, 1), (2, 2), (2, 3), (1, 0), (1, 1), (1, 2), (1, 3)]
 
         def piece(n):
-            if -2 <= n <= 0:
-                return (0, 1, n + 3, None)
-            b, j = divmod(n - 1, NT)
-            if n < 1 or b + 1 >= B:
+            if -3 <= n <= -1:
+                return (0, 1, n + 4, None)
+            b, j = divmod(n, NT)
+            if n < 0 or b + 1 >= B:
                 return None
             return (b + 1,) + PIECES[j] + (j,)
 
@@ -274,28 +295,31 @@ def tile_model_t_kernel(tc, x1, x2, out):
         prep_q(0, 2, 3)
 
         VW = 128
-        for n in range(-2, NQ + 3):
-            pn = piece(n)
-            pp = piece(n - 1)
+        for n in range(-3, NQ + 3):
+            p0 = piece(n)
+            p1 = piece(n - 1)
+            p2 = piece(n - 2)
             stage_g(n - 2)
             stage_c(n)
-            stage_r(n - 1)
-            if pp is not None:
-                prep_e(pp[0], pp[1], pp[2], "s" if pp[3] in PE_ON_SCALAR else "v")
+            stage_tot(n - 1)
+            if p1 is not None:
+                prep_e(p1[0], p1[1], p1[2], "s" if p1[3] in PE_ON_SCALAR else "v")
             stage_h(n - 2, "v")
-            if pp is not None and pp[3] is not None:
-                prep_vq(pp[0], pp[3], VW)
+            if p2 is not None and p2[3] is not None:
+                prep_vq(p2[0], p2[3], VW)
             if n == -1 or n == 0:
                 prep_vq(0, n + 1, 512)
-            if pn is not None and pn[3] is not None:
-                prep_vc(pn[0], pn[3], VW)
-            if pp is not None:
-                prep_q(pp[0], pp[1], pp[2])
+            if p2 is not None:
+                prep_q(p2[0], p2[1], p2[2])
             stage_a(n + 2)
             stage_d(n)
-            if pn is not None:
-                prep_t(pn[0], pn[1], pn[2], ps_x, "X")
+            if p0 is not None:
+                prep_t(p0[0], p0[1], p0[2], ps_x, "X")
             stage_e(n - 1)
             stage_f(n - 1)
+            stage_r(n - 1)
+            if p0 is not None and p0[3] is not None:
+                token(n - 1)
+                prep_vc(p0[0], p0[3], VW, "g")
             stage_h(n - 2, "s")
             stage_b(n + 2)

@@ -22,7 +22,7 @@ FLOPS = 2 * 2 * B * S * S * D
 
 MANUAL = True
 H_VECTOR_FROM = 24
-PE_ON_SCALAR = ()
+H_VECTOR_TILES = (2, 6)
 
 
 def tile_model_t_kernel(tc, x1, x2, out):
@@ -134,12 +134,12 @@ def tile_model_t_kernel(tc, x1, x2, out):
 
         st = {}
 
-        def stage_a(i):
+        def stage_a(i, halves=(0, 1)):
             if not 0 <= i < NQ:
                 return
             b, c = divmod(i, NT)
-            s = []
-            for h in range(2):
+            s = st.get(("s", i), [])
+            for h in halves:
                 sh = ps_s.tile([P, 512], F32, name="s%d" % h, tag="S%d" % h)
                 nc.tensor.matmul_mx(
                     out=sh[:],
@@ -182,6 +182,12 @@ def tile_model_t_kernel(tc, x1, x2, out):
             if not 0 <= i < NQ:
                 return
             e = st[("e", i)]
+            if i == NQ - 1:
+                halves = [ps_t.tile([P, 4, P], BF16, name="et_a", tag="T"), ps_s.tile([P, 4, P], BF16, name="et_b", tag="S0")]
+                for c in range(NT):
+                    nc.tensor.transpose(halves[c // 4][:, c % 4, :], e[:, P * c:P * (c + 1)], ident_b[:])
+                st[("et", i)] = halves
+                return
             et = ps_t.tile([P, NT, P], BF16, name="et", tag="T")
             for c in range(NT):
                 nc.tensor.transpose(et[:, c, :], e[:, P * c:P * (c + 1)], ident_b[:])
@@ -192,8 +198,12 @@ def tile_model_t_kernel(tc, x1, x2, out):
                 return
             et = st[("et", i)]
             eg = work.tile([P, 2, P, 4], BF16, name="eg", align_bytes=64)
-            nc.scalar.copy(out=eg[:], in_=et[:].rearrange("p (g t) q -> p g q t", g=2))
             st[("eg", i)] = eg
+            if i == NQ - 1:
+                nc.scalar.copy(out=eg[:, 0], in_=et[0][:].rearrange("p t q -> p q t"))
+                nc.vector.tensor_copy(out=eg[:, 1], in_=et[1][:].rearrange("p t q -> p q t"))
+                return
+            nc.scalar.copy(out=eg[:], in_=et[:].rearrange("p (g t) q -> p g q t", g=2))
 
         def stage_f(i):
             if not 0 <= i < NQ:
@@ -232,6 +242,21 @@ def tile_model_t_kernel(tc, x1, x2, out):
                 return
             b, c = divmod(i, NT)
             ec, es = st[("ec", i)]
+            if i == NQ - 1:
+                outs = [ps_x.tile([P, D // 2], F32, name="o_a", tag="X"), ps_s.tile([P, D // 2], F32, name="o_b", tag="S1")]
+                for dh in range(2):
+                    for g in range(2):
+                        nc.tensor.matmul_mx(
+                            out=outs[dh][:],
+                            lhsT=ec[:, P * g:P * (g + 1)].bitcast(FP8X4),
+                            lhsT_scale=es[:, P * g:P * (g + 1)],
+                            rhs=op(b, "cv")[:, g, 256 * dh:256 * (dh + 1)].bitcast(FP8X4),
+                            rhs_scale=op(b, "sv")[:, g, 256 * dh:256 * (dh + 1)],
+                            start=(g == 0),
+                            stop=(g == 1),
+                        )
+                st[("o", i)] = outs
+                return
             if i >= 25 and i % 2 == 1:
                 o = ps_x.tile([P, D], F32, name="o", tag="X")
             else:
@@ -248,8 +273,15 @@ def tile_model_t_kernel(tc, x1, x2, out):
                 )
             st[("o", i)] = o
 
+        def h_engine(i):
+            if i == NQ - 2:
+                return "s"
+            if i >= H_VECTOR_FROM or i % NT in H_VECTOR_TILES:
+                return "v"
+            return "s"
+
         def stage_h(i, eng):
-            if not 0 <= i < NQ or eng != ("v" if i >= H_VECTOR_FROM else "s"):
+            if not 0 <= i < NQ or (i < NQ - 1 and eng != h_engine(i)):
                 return
             b, c = divmod(i, NT)
             o = st[("o", i)]
@@ -257,6 +289,14 @@ def tile_model_t_kernel(tc, x1, x2, out):
             if c % 2 == 0:
                 st["osb"] = work.tile([P, 2, D], F32, name="osb")
             osb = st["osb"]
+            if i == NQ - 1:
+                if eng == "s":
+                    nc.scalar.activation(out=osb[:, 1, 0:256], in_=o[0][:], func=ACTF.Copy, scale=rs)
+                    nc.sync.dma_start(out=out_v[b][:, c, 0:256], in_=osb[:, 1, 0:256])
+                else:
+                    nc.vector.tensor_scalar(out=osb[:, 1, 256:512], in0=o[1][:], scalar1=rs, scalar2=None, op0=ALU.mult)
+                    nc.sync.dma_start(out=out_v[b][:, c, 256:512], in_=osb[:, 1, 256:512])
+                return
             if eng == "v":
                 nc.vector.tensor_scalar(out=osb[:, c % 2, :], in0=o[:], scalar1=rs, scalar2=None, op0=ALU.mult)
             else:
@@ -267,14 +307,38 @@ def tile_model_t_kernel(tc, x1, x2, out):
                 nc.sync.dma_start(out=out_v[b][:, c - 1:c + 1, :], in_=osb[:])
 
         PIECES = [(2, 0), (2, 1), (2, 2), (2, 3), (1, 0), (1, 1), (1, 2), (1, 3)]
+        VW = 128
 
-        def piece(n):
-            if -3 <= n <= -1:
-                return (0, 1, n + 4, None)
-            b, j = divmod(n, NT)
-            if n < 0 or b + 1 >= B:
+        def piece(m):
+            b, j = divmod(m, NT)
+            if m < 0 or b + 1 >= B:
                 return None
             return (b + 1,) + PIECES[j] + (j,)
+
+        def pt(m):
+            p = piece(m)
+            if p is not None:
+                prep_t(p[0], p[1], p[2], ps_x, "X")
+
+        def pe(m):
+            p = piece(m)
+            if p is not None:
+                prep_e(p[0], p[1], p[2], "v")
+
+        def pq(m):
+            p = piece(m)
+            if p is not None:
+                prep_q(p[0], p[1], p[2])
+
+        def vc(m):
+            p = piece(m)
+            if p is not None:
+                prep_vc(p[0], p[3], VW, "g")
+
+        def vq(m):
+            p = piece(m)
+            if p is not None:
+                prep_vq(p[0], p[3], VW)
 
         prep_t(0, 2, 0, ps_t, "T")
         prep_t(0, 2, 1, ps_t, "T")
@@ -290,36 +354,75 @@ def tile_model_t_kernel(tc, x1, x2, out):
         prep_q(0, 1, 0)
         prep_e(0, 2, 2, "s")
         prep_e(0, 2, 3, "s")
-        prep_vc(0, 1, 512, "s")
         prep_q(0, 2, 2)
         prep_q(0, 2, 3)
+        stage_a(0, (0,))
+        prep_t(0, 1, 1, ps_o, "O")
+        stage_a(0, (1,))
+        stage_a(1)
+        prep_t(0, 1, 2, ps_x, "X")
+        prep_t(0, 1, 3, ps_t, "T")
+        prep_vc(0, 2, 256, "s")
+        prep_e(0, 1, 1, "s")
+        prep_vc(0, 3, 256, "s")
+        stage_b(0)
+        prep_q(0, 1, 1)
+        stage_b(1)
+        prep_vq(0, 0, 512)
+        prep_vq(0, 1, 512)
+        stage_c(0)
+        prep_e(0, 1, 2, "s")
+        prep_q(0, 1, 2)
+        first_token = small.tile([P, 1], F32, name="first_token")
+        nc.vector.memset(first_token[:], 0.0)
+        tok0 = small.tile([P, 1], F32, name="tok")
+        nc.gpsimd.tensor_copy(out=tok0[:], in_=first_token[:])
+        vc(0)
+        stage_a(2)
+        stage_d(0)
+        pt(0)
+        stage_c(1)
+        prep_e(0, 1, 3, "s")
+        stage_b(2)
+        pe(0)
+        prep_q(0, 1, 3)
+        stage_a(3)
+        stage_d(1)
+        stage_tot(0)
+        stage_e(0)
+        stage_f(0)
+        stage_r(0)
+        token(0)
+        vc(1)
+        pt(1)
+        stage_b(3)
 
-        VW = 128
-        for n in range(-3, NQ + 3):
-            p0 = piece(n)
-            p1 = piece(n - 1)
-            p2 = piece(n - 2)
+        for n in range(2, NQ):
             stage_g(n - 2)
             stage_c(n)
             stage_tot(n - 1)
-            if p1 is not None:
-                prep_e(p1[0], p1[1], p1[2], "s" if p1[3] in PE_ON_SCALAR else "v")
+            pe(n - 1)
             stage_h(n - 2, "v")
-            if p2 is not None and p2[3] is not None:
-                prep_vq(p2[0], p2[3], VW)
-            if n == -1 or n == 0:
-                prep_vq(0, n + 1, 512)
-            if p2 is not None:
-                prep_q(p2[0], p2[1], p2[2])
+            vq(n - 2)
+            pq(n - 2)
             stage_a(n + 2)
             stage_d(n)
-            if p0 is not None:
-                prep_t(p0[0], p0[1], p0[2], ps_x, "X")
+            pt(n)
             stage_e(n - 1)
             stage_f(n - 1)
             stage_r(n - 1)
-            if p0 is not None and p0[3] is not None:
+            if piece(n) is not None:
                 token(n - 1)
-                prep_vc(p0[0], p0[3], VW, "g")
+                vc(n)
             stage_h(n - 2, "s")
             stage_b(n + 2)
+
+        stage_tot(NQ - 1)
+        stage_e(NQ - 1)
+        stage_f(NQ - 1)
+        stage_r(NQ - 1)
+        stage_g(NQ - 2)
+        stage_g(NQ - 1)
+        stage_h(NQ - 2, "s")
+        stage_h(NQ - 1, "s")
+        stage_h(NQ - 1, "v")

@@ -22,7 +22,7 @@ FLOPS = 2 * 2 * B * S * S * D
 
 MANUAL = True
 H_VECTOR_FROM = 24
-H_VECTOR_TILES = (2, 6)
+H_VECTOR_TILES = ()
 
 
 def tile_model_t_kernel(tc, x1, x2, out):

@@ -223,12 +223,6 @@ def tile_model_t_kernel(tc, x1, x2, out):
             nc.gpsimd.tensor_tensor(out=tot[:], in0=sm[:, 0:1], in1=sm[:, 1:2], op=ALU.add)
             st[("tot", i)] = tot
 
-        def token(i):
-            if not 0 <= i < NQ:
-                return
-            tok = small.tile([P, 1], F32, name="tok")
-            nc.gpsimd.tensor_copy(out=tok[:], in_=st[("rs", i)][:])
-
         def stage_r(i):
             if not 0 <= i < NQ:
                 return
@@ -373,10 +367,6 @@ def tile_model_t_kernel(tc, x1, x2, out):
         stage_c(0)
         prep_e(0, 1, 2, "s")
         prep_q(0, 1, 2)
-        first_token = small.tile([P, 1], F32, name="first_token")
-        nc.vector.memset(first_token[:], 0.0)
-        tok0 = small.tile([P, 1], F32, name="tok")
-        nc.gpsimd.tensor_copy(out=tok0[:], in_=first_token[:])
         vc(0)
         stage_a(2)
         stage_d(0)
@@ -392,7 +382,6 @@ def tile_model_t_kernel(tc, x1, x2, out):
         stage_e(0)
         stage_f(0)
         stage_r(0)
-        token(0)
         vc(1)
         pt(1)
         stage_b(3)
@@ -412,7 +401,6 @@ def tile_model_t_kernel(tc, x1, x2, out):
             stage_f(n - 1)
             stage_r(n - 1)
             if piece(n) is not None:
-                token(n - 1)
                 vc(n)
             stage_h(n - 2, "s")
             stage_b(n + 2)

from contextlib import ExitStack
import math

import concourse.mybir as mybir
from concourse.masks import make_identity

F32 = mybir.dt.float32
BF16 = mybir.dt.bfloat16
U32 = mybir.dt.uint32
U8 = mybir.dt.uint8
FP8X4 = mybir.dt.float8_e4m3fn_x4
ACTF = mybir.ActivationFunctionType
ALU = mybir.AluOpType
AX = mybir.AxisListType

B, S, D = 4, 1024, 512
P = 128
NT = S // P
NQ = B * NT
SCALE = 1.0 / math.sqrt(D)
FLOPS = 2 * 2 * B * S * S * D

MANUAL = True
H_VECTOR_FROM = 24
H_VECTOR_TILES = ()


def tile_model_t_kernel(tc, x1, x2, out):
    nc = tc.nc
    with ExitStack() as ctx:
        if MANUAL:
            ctx.enter_context(tc.manual_schedule())
        const = ctx.enter_context(tc.tile_pool(name="const", bufs=1))
        xin = ctx.enter_context(tc.tile_pool(name="xin", bufs=1))
        prep = ctx.enter_context(tc.tile_pool(name="prep", bufs=2))
        work = ctx.enter_context(tc.tile_pool(name="work", bufs=4))
        small = ctx.enter_context(tc.tile_pool(name="small", bufs=6))
        ps_s = ctx.enter_context(tc.psum_pool(name="ps_s", bufs=2))
        ps_t = ctx.enter_context(tc.psum_pool(name="ps_t", bufs=2))
        ps_o = ctx.enter_context(tc.psum_pool(name="ps_o", bufs=1))
        ps_x = ctx.enter_context(tc.psum_pool(name="ps_x", bufs=1))

        x1_sb = []
        x2_sb = []
        for b in range(B):
            t2 = xin.tile([P, NT, D], BF16, name="x2_sb%d" % b)
            t1 = xin.tile([P, NT, D], BF16, name="x1_sb%d" % b)
            x2_sb.append(t2)
            x1_sb.append(t1)
        for b in range(B):
            v2 = x2[b].rearrange("(g p t) d -> p g t d", g=2, t=4)
            v1 = x1[b].rearrange("(p c) d -> p c d", c=NT)
            if b == 0:
                nc.sync.dma_start(out=x2_sb[b][:, 0:2, :], in_=v2[:, 0, 0:2, :])
                nc.sync.dma_start(out=x2_sb[b][:, 2:4, :], in_=v2[:, 0, 2:4, :])
                nc.sync.dma_start(out=x1_sb[b][:, 0:2, :], in_=v1[:, 0:2, :])
                nc.sync.dma_start(out=x2_sb[b][:, 4:6, :], in_=v2[:, 1, 0:2, :])
                nc.sync.dma_start(out=x2_sb[b][:, 6:8, :], in_=v2[:, 1, 2:4, :])
                nc.sync.dma_start(out=x1_sb[b][:, 2:8, :], in_=v1[:, 2:8, :])
            else:
                nc.sync.dma_start(out=x2_sb[b][:, 0:4, :], in_=v2[:, 0])
                nc.sync.dma_start(out=x2_sb[b][:, 4:8, :], in_=v2[:, 1])
                nc.sync.dma_start(out=x1_sb[b][:], in_=v1)
        out_v = [out[b].rearrange("(p c) d -> p c d", c=NT) for b in range(B)]

        ident_f = const.tile([P, P], F32, name="ident_f")
        make_identity(nc, ident_f[:])
        ident_b = const.tile([P, P], BF16, name="ident_b")
        make_identity(nc, ident_b[:])

        ops = {}
        SHAPES = {
            "g1": ([P, 4 * S], BF16), "g2": ([P, 4 * S], BF16), "gv": ([P, 2, D, 4], BF16),
            "c1": ([P, S], U32), "c2": ([P, S], U32), "cv": ([P, 2, D], U32),
            "s1": ([P, S], U8), "s2": ([P, S], U8), "sv": ([P, 2, D], U8),
        }

        def op(b, key):
            if (b, key) not in ops:
                shape, dt = SHAPES[key]
                ops[(b, key)] = prep.tile(shape, dt, name=key, align_bytes=64)
            return ops[(b, key)]

        xts = {}

        def prep_t(b, which, k, pool, tag):
            src = x1_sb[b] if which == 1 else x2_sb[b]
            xt = pool.tile([P, 2, 2, P], F32, name="xt", tag=tag)
            for r in range(2):
                words = src[:, 2 * k + r, :].bitcast(F32)
                for u in range(2):
                    nc.tensor.transpose(xt[:, r, u, :], words[:, P * u:P * (u + 1)], ident_f[:])
            xts[(b, which, k)] = xt

        def prep_e(b, which, k, eng):
            xt = xts[(b, which, k)]
            grouped = op(b, "g%d" % which)
            dst = grouped[:, 1024 * k:1024 * (k + 1)].bitcast(F32).rearrange("p (r j u) -> p r j u", r=2, u=2)
            srcv = xt[:].rearrange("p r u j -> p r j u")
            if eng == "v":
                nc.vector.tensor_copy(out=dst, in_=srcv)
            else:
                nc.scalar.copy(out=dst, in_=srcv)

        def prep_q(b, which, k):
            nc.vector.quantize_mx(
                out=op(b, "c%d" % which)[:, 256 * k:256 * (k + 1)].bitcast(FP8X4),
                scales=op(b, "s%d" % which)[:, 256 * k:256 * (k + 1)],
                in_=op(b, "g%d" % which)[:, 1024 * k:1024 * (k + 1)],
            )

        def prep_vc(b, j, w, eng="v"):
            g, lo = divmod(j * w, D)
            dst = op(b, "gv")[:, g, lo:lo + w, :].rearrange("p (c i) t -> p c t i", i=4)
            srcv = x2_sb[b][:, 4 * g:4 * g + 4, lo:lo + w].rearrange("p t (c i) -> p c t i", i=4)
            if eng == "v":
                nc.vector.tensor_copy(out=dst, in_=srcv)
            elif eng == "s":
                nc.scalar.copy(out=dst, in_=srcv)
            else:
                nc.gpsimd.tensor_scalar(
                    out=op(b, "gv")[:, g, lo:lo + w, :],
                    in0=x2_sb[b][:, 4 * g:4 * g + 4, lo:lo + w].rearrange("p t d -> p d t"),
                    scalar1=1.0, scalar2=0.0, op0=ALU.mult, op1=ALU.add,
                )

        def prep_vq(b, j, w):
            g, lo = divmod(j * w, D)
            nc.vector.quantize_mx(
                out=op(b, "cv")[:, g, lo:lo + w].bitcast(FP8X4),
                scales=op(b, "sv")[:, g, lo:lo + w],
                in_=op(b, "gv")[:, g, lo:lo + w, :].rearrange("p d t -> p (d t)"),
            )

        st = {}

        def stage_a(i, halves=(0, 1)):
            if not 0 <= i < NQ:
                return
            b, c = divmod(i, NT)
            s = st.get(("s", i), [])
            for h in halves:
                sh = ps_s.tile([P, 512], F32, name="s%d" % h, tag="S%d" % h)
                nc.tensor.matmul_mx(
                    out=sh[:],
                    lhsT=op(b, "c1")[:, P * c:P * (c + 1)].bitcast(FP8X4),
                    lhsT_scale=op(b, "s1")[:, P * c:P * (c + 1)],
                    rhs=op(b, "c2")[:, 512 * h:512 * (h + 1)].bitcast(FP8X4),
                    rhs_scale=op(b, "s2")[:, 512 * h:512 * (h + 1)],
                    start=True,
                    stop=True,
                )
                s.append(sh)
            st[("s", i)] = s

        def stage_b(i):
            if not 0 <= i < NQ:
                return
            s = st[("s", i)]
            mx = small.tile([P, 2], F32, name="mx")
            for h in range(2):
                nc.vector.reduce_max(out=mx[:, h:h + 1], in_=s[h][:], axis=AX.X)
            nm = small.tile([P, 1], F32, name="nm")
            nc.vector.tensor_scalar(out=nm[:], in0=mx[:, 0:1], scalar1=mx[:, 1:2], scalar2=-SCALE,
                                    op0=ALU.max, op1=ALU.mult)
            st[("nm", i)] = nm

        def stage_c(i):
            if not 0 <= i < NQ:
                return
            s = st[("s", i)]
            nm = st[("nm", i)]
            e = work.tile([P, S], BF16, name="e")
            sm = small.tile([P, 2], F32, name="sm")
            for h in range(2):
                nc.scalar.activation(out=e[:, 512 * h:512 * (h + 1)], in_=s[h][:], func=ACTF.Exp,
                                     bias=nm[:], scale=SCALE, accum_out=sm[:, h:h + 1])
            st[("e", i)] = e
            st[("sm", i)] = sm

        def stage_d(i):
            if not 0 <= i < NQ:
                return
            e = st[("e", i)]
            if i == NQ - 1:
                halves = [ps_t.tile([P, 4, P], BF16, name="et_a", tag="T"), ps_s.tile([P, 4, P], BF16, name="et_b", tag="S0")]
                for c in range(NT):
                    nc.tensor.transpose(halves[c // 4][:, c % 4, :], e[:, P * c:P * (c + 1)], ident_b[:])
                st[("et", i)] = halves
                return
            et = ps_t.tile([P, NT, P], BF16, name="et", tag="T")
            for c in range(NT):
                nc.tensor.transpose(et[:, c, :], e[:, P * c:P * (c + 1)], ident_b[:])
            st[("et", i)] = et

        def stage_e(i):
            if not 0 <= i < NQ:
                return
            et = st[("et", i)]
            eg = work.tile([P, 2, P, 4], BF16, name="eg", align_bytes=64)
            st[("eg", i)] = eg
            if i == NQ - 1:
                nc.scalar.copy(out=eg[:, 0], in_=et[0][:].rearrange("p t q -> p q t"))
                nc.vector.tensor_copy(out=eg[:, 1], in_=et[1][:].rearrange("p t q -> p q t"))
                return
            nc.scalar.copy(out=eg[:], in_=et[:].rearrange("p (g t) q -> p g q t", g=2))

        def stage_f(i):
            if not 0 <= i < NQ:
                return
            eg = st[("eg", i)]
            ec = work.tile([P, 2 * P], U32, name="ec", align_bytes=64)
            es = work.tile([P, 2 * P], U8, name="es", align_bytes=64)
            nc.vector.quantize_mx(out=ec[:].bitcast(FP8X4), scales=es[:],
                                  in_=eg[:].rearrange("p g q t -> p (g q t)"))
            st[("ec", i)] = (ec, es)

        def stage_tot(i):
            if not 0 <= i < NQ:
                return
            sm = st[("sm", i)]
            tot = small.tile([P, 1], F32, name="tot")
            nc.gpsimd.tensor_tensor(out=tot[:], in0=sm[:, 0:1], in1=sm[:, 1:2], op=ALU.add)
            st[("tot", i)] = tot

        def stage_r(i):
            if not 0 <= i < NQ:
                return
            tot = st[("tot", i)]
            rs = small.tile([P, 1], F32, name="rs")
            nc.vector.reciprocal(out=rs[:], in_=tot[:])
            st[("rs", i)] = rs

        def stage_g(i):
            if not 0 <= i < NQ:
                return
            b, c = divmod(i, NT)
            ec, es = st[("ec", i)]
            if i == NQ - 1:
                outs = [ps_x.tile([P, D // 2], F32, name="o_a", tag="X"), ps_s.tile([P, D // 2], F32, name="o_b", tag="S1")]
                for dh in range(2):
                    for g in range(2):
                        nc.tensor.matmul_mx(
                            out=outs[dh][:],
                            lhsT=ec[:, P * g:P * (g + 1)].bitcast(FP8X4),
                            lhsT_scale=es[:, P * g:P * (g + 1)],
                            rhs=op(b, "cv")[:, g, 256 * dh:256 * (dh + 1)].bitcast(FP8X4),
                            rhs_scale=op(b, "sv")[:, g, 256 * dh:256 * (dh + 1)],
                            start=(g == 0),
                            stop=(g == 1),
                        )
                st[("o", i)] = outs
                return
            if i >= 25 and i % 2 == 1:
                o = ps_x.tile([P, D], F32, name="o", tag="X")
            else:
                o = ps_o.tile([P, D], F32, name="o", tag="O")
            for g in range(2):
                nc.tensor.matmul_mx(
                    out=o[:],
                    lhsT=ec[:, P * g:P * (g + 1)].bitcast(FP8X4),
                    lhsT_scale=es[:, P * g:P * (g + 1)],
                    rhs=op(b, "cv")[:, g, :].bitcast(FP8X4),
                    rhs_scale=op(b, "sv")[:, g, :],
                    start=(g == 0),
                    stop=(g == 1),
                )
            st[("o", i)] = o

        def h_engine(i):
            if i == NQ - 2:
                return "s"
            if i >= H_VECTOR_FROM or i % NT in H_VECTOR_TILES:
                return "v"
            return "s"

        def stage_h(i, eng):
            if not 0 <= i < NQ or (i < NQ - 1 and eng != h_engine(i)):
                return
            b, c = divmod(i, NT)
            o = st[("o", i)]
            rs = st[("rs", i)][:]
            if c % 2 == 0:
                st["osb"] = work.tile([P, 2, D], F32, name="osb")
            osb = st["osb"]
            if i == NQ - 1:
                if eng == "s":
                    nc.scalar.activation(out=osb[:, 1, 0:256], in_=o[0][:], func=ACTF.Copy, scale=rs)
                    nc.sync.dma_start(out=out_v[b][:, c, 0:256], in_=osb[:, 1, 0:256])
                else:
                    nc.vector.tensor_scalar(out=osb[:, 1, 256:512], in0=o[1][:], scalar1=rs, scalar2=None, op0=ALU.mult)
                    nc.sync.dma_start(out=out_v[b][:, c, 256:512], in_=osb[:, 1, 256:512])
                return
            if eng == "v":
                nc.vector.tensor_scalar(out=osb[:, c % 2, :], in0=o[:], scalar1=rs, scalar2=None, op0=ALU.mult)
            else:
                nc.scalar.activation(out=osb[:, c % 2, :], in_=o[:], func=ACTF.Copy, scale=rs)
            if i >= NQ - 2:
                nc.sync.dma_start(out=out_v[b][:, c, :], in_=osb[:, c % 2, :])
            elif c % 2 == 1:
                nc.sync.dma_start(out=out_v[b][:, c - 1:c + 1, :], in_=osb[:])

        PIECES = [(2, 0), (2, 1), (2, 2), (2, 3), (1, 0), (1, 1), (1, 2), (1, 3)]
        VW = 128

        def piece(m):
            b, j = divmod(m, NT)
            if m < 0 or b + 1 >= B:
                return None
            return (b + 1,) + PIECES[j] + (j,)

        def pt(m):
            p = piece(m)
            if p is not None:
                prep_t(p[0], p[1], p[2], ps_x, "X")

        def pe(m):
            p = piece(m)
            if p is not None:
                prep_e(p[0], p[1], p[2], "v")

        def pq(m):
            p = piece(m)
            if p is not None:
                prep_q(p[0], p[1], p[2])

        def vc(m):
            p = piece(m)
            if p is not None:
                prep_vc(p[0], p[3], VW, "g")

        def vq(m):
            p = piece(m)
            if p is not None:
                prep_vq(p[0], p[3], VW)

        prep_t(0, 2, 0, ps_t, "T")
        prep_t(0, 2, 1, ps_t, "T")
        prep_t(0, 1, 0, ps_o, "O")
        prep_t(0, 2, 2, ps_s, "S0")
        prep_t(0, 2, 3, ps_s, "S1")
        prep_vc(0, 0, 512, "v")
        prep_e(0, 2, 0, "s")
        prep_e(0, 2, 1, "v")
        prep_e(0, 1, 0, "s")
        prep_q(0, 2, 0)
        prep_q(0, 2, 1)
        prep_q(0, 1, 0)
        prep_e(0, 2, 2, "s")
        prep_e(0, 2, 3, "s")
        prep_q(0, 2, 2)
        prep_q(0, 2, 3)
        stage_a(0, (0,))
        prep_t(0, 1, 1, ps_o, "O")
        stage_a(0, (1,))
        stage_a(1)
        prep_t(0, 1, 2, ps_x, "X")
        prep_t(0, 1, 3, ps_t, "T")
        prep_vc(0, 2, 256, "s")
        prep_e(0, 1, 1, "s")
        prep_vc(0, 3, 256, "s")
        stage_b(0)
        prep_q(0, 1, 1)
        stage_b(1)
        prep_vq(0, 0, 512)
        prep_vq(0, 1, 512)
        stage_c(0)
        prep_e(0, 1, 2, "s")
        prep_q(0, 1, 2)
        vc(0)
        stage_a(2)
        stage_d(0)
        pt(0)
        stage_c(1)
        prep_e(0, 1, 3, "s")
        stage_b(2)
        pe(0)
        prep_q(0, 1, 3)
        stage_a(3)
        stage_d(1)
        stage_tot(0)
        stage_e(0)
        stage_f(0)
        stage_r(0)
        vc(1)
        pt(1)
        stage_b(3)

        for n in range(2, NQ):
            stage_g(n - 2)
            stage_c(n)
            stage_tot(n - 1)
            pe(n - 1)
            stage_h(n - 2, "v")
            vq(n - 2)
            pq(n - 2)
            stage_a(n + 2)
            stage_d(n)
            pt(n)
            stage_e(n - 1)
            stage_f(n - 1)
            stage_r(n - 1)
            if piece(n) is not None:
                vc(n)
            stage_h(n - 2, "s")
            stage_b(n + 2)

        stage_tot(NQ - 1)
        stage_e(NQ - 1)
        stage_f(NQ - 1)
        stage_r(NQ - 1)
        stage_g(NQ - 2)
        stage_g(NQ - 1)
        stage_h(NQ - 2, "s")
        stage_h(NQ - 1, "s")
        stage_h(NQ - 1, "v")
